import numpy as np
import ml_dtypes


def mxq(x, axis, fmt="e4m3"):
    dtype, down = {"e4m3": (ml_dtypes.float8_e4m3fn, 7), "e5m2": (ml_dtypes.float8_e5m2, 14)}[fmt]
    v = np.moveaxis(np.asarray(x, np.float32).astype(ml_dtypes.bfloat16).astype(np.float64), axis, -1)
    blocks = v.reshape(v.shape[:-1] + (-1, 32))
    amax = np.abs(blocks).max(-1, keepdims=True)
    byte = np.maximum(np.where(amax > 0, np.frexp(amax)[1] - 1 + 127, 0) - down, 1)
    scale = np.exp2(byte - 127.0)
    codes = (blocks / scale).astype(np.float32).astype(dtype).astype(np.float64)
    return np.moveaxis((codes * scale).reshape(v.shape), -1, axis)


WIDE = False


def mx_kscale(k):
    if not WIDE:
        return np.ones(k)
    levels = np.array([10, -10, 5, -5, 0])
    a = np.random.permutation(np.resize(levels, k // 512 * 4)).reshape(k // 512, 4)
    idx = np.arange(k)
    return np.exp2(a[idx // 512, idx % 128 // 32])


BF16 = ml_dtypes.bfloat16


def bf(x):
    return np.asarray(x, np.float32).astype(BF16)


def f64(x):
    return np.asarray(x).astype(np.float64)


B, IDIM, HDIM, ODIM, S, DEPTH, NACT, NTOP = 128, 512, 512, 128, 128, 32, 3, 2


def sigmoid(v):
    return 1.0 / (1.0 + np.exp(-v))


def setup_inputs():
    s = mx_kscale(HDIM)
    return {"h": bf(sigmoid(np.random.standard_normal((B, HDIM)) * 1.3) * s),
            "stack": bf(np.random.standard_normal((B, DEPTH, S))),
            "Wa": bf(np.random.standard_normal((NACT * S, HDIM)) * 3.0 / np.sqrt(HDIM) / s),
            "ba": bf(np.random.standard_normal(NACT * S) * 0.5),
            "Ws": bf(np.random.standard_normal((S, HDIM)) * 2.0 / np.sqrt(HDIM) / s),
            "bs": bf(np.random.standard_normal(S)),
            "Wo": bf(np.random.standard_normal((ODIM, HDIM)) * 2.0 / np.sqrt(HDIM) / s),
            "bo": bf(np.random.standard_normal(ODIM) * 0.3)}


def reference(h, stack, Wa, ba, Ws, bs, Wo, bo):
    st = f64(stack)
    hq = mxq(f64(h), 1, "e4m3")
    logits = ((hq @ mxq(f64(Wa), 1, "e4m3").T) + f64(ba)).reshape(-1, NACT, S)
    e = np.exp(logits - logits.max(axis=1, keepdims=True))
    act = e / e.sum(axis=1, keepdims=True)
    top = sigmoid((hq @ mxq(f64(Ws), 1, "e4m3").T) + f64(bs))[:, None, :]
    push = np.concatenate([top, st[:, :-1]], axis=1)
    empty = np.full((st.shape[0], 1, S), -1.0)
    pop = np.concatenate([st[:, 1:], empty], axis=1)
    new_stack = (push * act[:, 0][:, None, :]
                 + pop * act[:, 1][:, None, :]
                 + st * act[:, 2][:, None, :])
    out = (hq @ mxq(f64(Wo), 1, "e4m3").T) + f64(bo)
    return out, new_stack

@@ -1,0 +1,210 @@
+from contextlib import ExitStack
+
+import concourse.masks as masks
+import concourse.mybir as mybir
+
+F32 = mybir.dt.float32
+BF16 = mybir.dt.bfloat16
+U32 = mybir.dt.uint32
+U8 = mybir.dt.uint8
+FP8X4 = mybir.dt.float8_e4m3fn_x4
+ACT = mybir.ActivationFunctionType
+ALU = mybir.AluOpType
+
+P = 128
+HDIM = 512
+DEPTH = 32
+WORDS = HDIM // 2
+HALVES = 2
+PACK = 4
+
+H_BLOCK = 0
+PUSH, POP, NOOP, TOP, OUT = 0, 1, 2, 3, 4
+OPERANDS = 6
+PAIRS = OPERANDS // 2
+
+SLICES_PER_BANK = 8
+STACK_BANKS = DEPTH // SLICES_PER_BANK
+CHUNK = 4
+CHUNKS = DEPTH // CHUNK
+
+FLOPS = 2 * P * HDIM * (3 * P + P + P)
+
+
+def tile_stackrnn_pb_s_kernel(tc, h, stack, Wa, ba, Ws, bs, Wo, bo, out_0, out_1):
+    nc = tc.nc
+    with ExitStack() as ctx:
+        ctx.enter_context(tc.manual_schedule())
+        keep = ctx.enter_context(tc.tile_pool(name="keep", bufs=1))
+        staging = ctx.enter_context(tc.tile_pool(name="staging", bufs=4))
+        psum_stack = ctx.enter_context(tc.psum_pool(name="psum_stack", bufs=1))
+        psum_work = ctx.enter_context(tc.psum_pool(name="psum_work", bufs=4))
+
+        operands = keep.tile([P, OPERANDS, HDIM], BF16)
+        nc.sync.dma_start(out=operands[:, H_BLOCK, :], in_=h)
+        nc.sync.dma_start(
+            out=operands[:, 1 + PUSH : 1 + TOP, :], in_=Wa.rearrange("(j n) k -> n j k", n=P)
+        )
+        nc.sync.dma_start(out=operands[:, 1 + TOP, :], in_=Ws)
+        nc.sync.dma_start(out=operands[:, 1 + OUT, :], in_=Wo)
+        stack_sb = keep.tile([P, DEPTH, P], BF16)
+        for bank in range(STACK_BANKS):
+            rows = slice(bank * SLICES_PER_BANK, (bank + 1) * SLICES_PER_BANK)
+            nc.sync.dma_start(out=stack_sb[:, rows, :], in_=stack[:, rows, :])
+
+        bias_rows = keep.tile([P, P], BF16)
+        nc.vector.memset(bias_rows[:], 0.0)
+        nc.scalar.dma_start(out=bias_rows[PUSH : NOOP + 1, :], in_=ba.rearrange("(j n) -> j n", n=P))
+        nc.scalar.dma_start(out=bias_rows[TOP : TOP + 1, :], in_=bs.rearrange("(o n) -> o n", o=1))
+        nc.scalar.dma_start(out=bias_rows[OUT : OUT + 1, :], in_=bo.rearrange("(o n) -> o n", o=1))
+
+        warm = keep.tile([P, 1], F32)
+        nc.vector.memset(warm[:], 0.0)
+        nc.scalar.activation(out=warm[:], in_=warm[:], func=ACT.Exp)
+
+        ident_f32 = keep.tile([P, P], F32)
+        masks.make_identity(nc, ident_f32[:])
+        ident_bf16 = keep.tile([P, P], BF16)
+        masks.make_identity(nc, ident_bf16[:])
+
+        grouped = keep.tile([P, OPERANDS, P, PACK], BF16, align_bytes=64)
+        grouped_words = grouped[:].bitcast(F32)
+        codes = keep.tile([P, OPERANDS * P], U32, align_bytes=64)
+        scales = keep.tile([P, OPERANDS * P], U8, align_bytes=64)
+        for pair in range(PAIRS):
+            turned = psum_work.tile([P, 2, HALVES, P], F32, tag="work")
+            for i in range(2):
+                words = operands[:, 2 * pair + i, :].bitcast(F32)
+                for u in range(HALVES):
+                    nc.tensor.transpose(
+                        out=turned[:, i, u, :], in_=words[:, u * P : (u + 1) * P], identity=ident_f32[:]
+                    )
+            copy_out = nc.scalar.copy if pair % 2 == 0 else nc.vector.tensor_copy
+            copy_out(
+                out=grouped_words[:, 2 * pair : 2 * pair + 2, :, :],
+                in_=turned[:].rearrange("p i u r -> p i r u"),
+            )
+
+        bias_turned = psum_work.tile([P, P], BF16, tag="work")
+        nc.tensor.transpose(out=bias_turned[:], in_=bias_rows[:], identity=ident_bf16[:])
+        bias = keep.tile([P, OUT + 1], F32)
+        nc.vector.tensor_copy(out=bias[:], in_=bias_turned[:, 0 : OUT + 1])
+
+        for pair in range(PAIRS):
+            cols = slice(2 * pair * P, (2 * pair + 2) * P)
+            nc.vector.quantize_mx(
+                out=codes[:, cols].bitcast(FP8X4),
+                scales=scales[:, cols],
+                in_=grouped[:, 2 * pair : 2 * pair + 2, :, :].rearrange("p o r t -> p (o r t)"),
+            )
+
+        gates = psum_work.tile([P, TOP + 1, P], F32, tag="work")
+        readout = psum_work.tile([P, P], F32, tag="work")
+        h_cols = slice(H_BLOCK * P, (H_BLOCK + 1) * P)
+        for j in range(OUT + 1):
+            w_cols = slice((1 + j) * P, (2 + j) * P)
+            nc.tensor.matmul_mx(
+                out=readout[:] if j == OUT else gates[:, j, :],
+                lhsT=codes[:, w_cols].bitcast(FP8X4),
+                lhsT_scale=scales[:, w_cols],
+                rhs=codes[:, h_cols].bitcast(FP8X4),
+                rhs_scale=scales[:, h_cols],
+                start=True,
+                stop=True,
+            )
+
+        stack_turned = []
+        for bank in range(STACK_BANKS):
+            turned_bank = psum_stack.tile([P, SLICES_PER_BANK, P], BF16, name="stack_turned%d" % bank)
+            for i in range(SLICES_PER_BANK):
+                nc.tensor.transpose(
+                    out=turned_bank[:, i, :],
+                    in_=stack_sb[:, bank * SLICES_PER_BANK + i, :],
+                    identity=ident_bf16[:],
+                )
+            stack_turned.append(turned_bank)
+
+        out_turned = keep.tile([P, P], F32)
+        nc.scalar.activation(
+            out=out_turned[:], in_=readout[:], func=ACT.Identity, bias=bias[:, OUT : OUT + 1]
+        )
+
+        logits = keep.tile([P, 3, P], F32)
+        nc.vector.tensor_tensor(
+            out=logits[:],
+            in0=gates[:, PUSH : NOOP + 1, :],
+            in1=bias[:, PUSH : NOOP + 1].unsqueeze(2).to_broadcast([P, 3, P]),
+            op=ALU.add,
+        )
+        peak = keep.tile([P, P], F32)
+        nc.vector.tensor_max(out=peak[:], in0=logits[:, PUSH, :], in1=logits[:, POP, :])
+        nc.vector.tensor_max(out=peak[:], in0=peak[:], in1=logits[:, NOOP, :])
+        nc.vector.tensor_tensor(
+            out=logits[:],
+            in0=logits[:],
+            in1=peak[:].unsqueeze(1).to_broadcast([P, 3, P]),
+            op=ALU.subtract,
+        )
+        weight = keep.tile([P, 3, P], F32)
+        nc.scalar.activation(out=weight[:], in_=logits[:], func=ACT.Exp)
+        total = keep.tile([P, P], F32)
+        nc.vector.tensor_add(out=total[:], in0=weight[:, PUSH, :], in1=weight[:, POP, :])
+        nc.vector.tensor_add(out=total[:], in0=total[:], in1=weight[:, NOOP, :])
+        nc.vector.reciprocal(out=total[:], in_=total[:])
+        nc.vector.tensor_tensor(
+            out=weight[:],
+            in0=weight[:],
+            in1=total[:].unsqueeze(1).to_broadcast([P, 3, P]),
+            op=ALU.mult,
+        )
+
+        top = keep.tile([P, P], F32)
+        nc.scalar.activation(
+            out=top[:], in_=gates[:, TOP, :], func=ACT.Sigmoid, bias=bias[:, TOP : TOP + 1]
+        )
+
+        out_bank = psum_work.tile([P, P], F32, tag="work")
+        nc.tensor.transpose(out=out_bank[:], in_=out_turned[:], identity=ident_f32[:])
+        out_sb = keep.tile([P, P], F32)
+        nc.scalar.copy(out=out_sb[:], in_=out_bank[:])
+        nc.sync.dma_start(out=out_0, in_=out_sb[:])
+
+        pushed = keep.tile([P, DEPTH + 1, P], F32)
+        popped = keep.tile([P, DEPTH + 1, P], F32)
+        stayed = keep.tile([P, DEPTH, P], F32)
+        nc.vector.tensor_mul(out=pushed[:, 0, :], in0=weight[:, PUSH, :], in1=top[:])
+        nc.vector.tensor_scalar_mul(out=popped[:, DEPTH, :], in0=weight[:, POP, :], scalar1=-1.0)
+
+        def multiply(product, first_slot, action, chunk):
+            bank, half = divmod(chunk, SLICES_PER_BANK // CHUNK)
+            nc.vector.tensor_tensor(
+                out=product[:, first_slot : first_slot + CHUNK, :],
+                in0=stack_turned[bank][:, half * CHUNK : (half + 1) * CHUNK, :],
+                in1=weight[:, action, :].unsqueeze(1).to_broadcast([P, CHUNK, P]),
+                op=ALU.mult,
+            )
+
+        multiply(popped, 0, POP, 0)
+        for chunk in range(CHUNKS):
+            first = chunk * CHUNK
+            multiply(stayed, first, NOOP, chunk)
+            multiply(pushed, first + 1, PUSH, chunk)
+            if chunk + 1 < CHUNKS:
+                multiply(popped, first + CHUNK, POP, chunk + 1)
+
+            blended = psum_work.tile([P, CHUNK, P], F32, tag="work")
+            for i in range(CHUNK):
+                d = first + i
+                terms = [popped[:, d + 1, :], stayed[:, d, :], pushed[:, d, :]]
+                for n, term in enumerate(terms):
+                    nc.tensor.matmul(
+                        out=blended[:, i, :],
+                        lhsT=term,
+                        rhs=ident_f32[:],
+                        is_transpose=True,
+                        start=(n == 0),
+                        stop=(n == len(terms) - 1),
+                    )
+            new_rows = staging.tile([P, CHUNK, P], F32)
+            nc.scalar.copy(out=new_rows[:], in_=blended[:])
+            nc.sync.dma_start(out=out_1[:, first : first + CHUNK, :], in_=new_rows[:])

@@ -113,6 +113,7 @@ def tile_stackrnn_pb_s_kernel(tc, h, stack, Wa, ba, Ws, bs, Wo, bo, out_0, out_1
                 stop=True,
             )
 
+        stack_turned_sb = keep.tile([P, DEPTH, P], BF16)
         stack_turned = []
         for bank in range(STACK_BANKS):
             turned_bank = psum_stack.tile([P, SLICES_PER_BANK, P], BF16, name="stack_turned%d" % bank)
@@ -124,10 +125,15 @@ def tile_stackrnn_pb_s_kernel(tc, h, stack, Wa, ba, Ws, bs, Wo, bo, out_0, out_1
                 )
             stack_turned.append(turned_bank)
 
+        def copy_turned_bank(bank):
+            rows = slice(bank * SLICES_PER_BANK, (bank + 1) * SLICES_PER_BANK)
+            nc.scalar.copy(out=stack_turned_sb[:, rows, :], in_=stack_turned[bank][:])
+
         out_turned = keep.tile([P, P], F32)
         nc.scalar.activation(
             out=out_turned[:], in_=readout[:], func=ACT.Identity, bias=bias[:, OUT : OUT + 1]
         )
+        copy_turned_bank(0)
 
         logits = keep.tile([P, 3, P], F32)
         nc.vector.tensor_tensor(
@@ -162,6 +168,8 @@ def tile_stackrnn_pb_s_kernel(tc, h, stack, Wa, ba, Ws, bs, Wo, bo, out_0, out_1
         nc.scalar.activation(
             out=top[:], in_=gates[:, TOP, :], func=ACT.Sigmoid, bias=bias[:, TOP : TOP + 1]
         )
+        for bank in range(1, STACK_BANKS):
+            copy_turned_bank(bank)
 
         out_bank = psum_work.tile([P, P], F32, tag="work")
         nc.tensor.transpose(out=out_bank[:], in_=out_turned[:], identity=ident_f32[:])
@@ -176,10 +184,16 @@ def tile_stackrnn_pb_s_kernel(tc, h, stack, Wa, ba, Ws, bs, Wo, bo, out_0, out_1
         nc.vector.tensor_scalar_mul(out=popped[:, DEPTH, :], in0=weight[:, POP, :], scalar1=-1.0)
 
         def multiply(product, first_slot, action, chunk):
-            bank, half = divmod(chunk, SLICES_PER_BANK // CHUNK)
-            nc.vector.tensor_tensor(
+            if action == NOOP:
+                engine = nc.gpsimd
+                rows = stack_turned_sb[:, chunk * CHUNK : (chunk + 1) * CHUNK, :]
+            else:
+                engine = nc.vector
+                bank, half = divmod(chunk, SLICES_PER_BANK // CHUNK)
+                rows = stack_turned[bank][:, half * CHUNK : (half + 1) * CHUNK, :]
+            engine.tensor_tensor(
                 out=product[:, first_slot : first_slot + CHUNK, :],
-                in0=stack_turned[bank][:, half * CHUNK : (half + 1) * CHUNK, :],
+                in0=rows,
                 in1=weight[:, action, :].unsqueeze(1).to_broadcast([P, CHUNK, P]),
                 op=ALU.mult,
             )

@@ -10,23 +10,25 @@ U8 = mybir.dt.uint8
 FP8X4 = mybir.dt.float8_e4m3fn_x4
 ACT = mybir.ActivationFunctionType
 ALU = mybir.AluOpType
+AXIS = mybir.AxisListType
 
 P = 128
 HDIM = 512
 DEPTH = 32
-WORDS = HDIM // 2
 HALVES = 2
 PACK = 4
 
 H_BLOCK = 0
 PUSH, POP, NOOP, TOP, OUT = 0, 1, 2, 3, 4
 OPERANDS = 6
-PAIRS = OPERANDS // 2
 
+PSUM_BANKS = 8
 SLICES_PER_BANK = 8
 STACK_BANKS = DEPTH // SLICES_PER_BANK
 CHUNK = 4
 CHUNKS = DEPTH // CHUNK
+STEPS = DEPTH + 1
+AHEAD = 4
 
 FLOPS = 2 * P * HDIM * (3 * P + P + P)
 
@@ -37,20 +39,18 @@ def tile_stackrnn_pb_s_kernel(tc, h, stack, Wa, ba, Ws, bs, Wo, bo, out_0, out_1
         ctx.enter_context(tc.manual_schedule())
         keep = ctx.enter_context(tc.tile_pool(name="keep", bufs=1))
         staging = ctx.enter_context(tc.tile_pool(name="staging", bufs=4))
-        psum_stack = ctx.enter_context(tc.psum_pool(name="psum_stack", bufs=1))
-        psum_work = ctx.enter_context(tc.psum_pool(name="psum_work", bufs=4))
+        psum = ctx.enter_context(tc.psum_pool(name="psum", bufs=PSUM_BANKS))
 
         operands = keep.tile([P, OPERANDS, HDIM], BF16)
         nc.sync.dma_start(out=operands[:, H_BLOCK, :], in_=h)
-        nc.sync.dma_start(
-            out=operands[:, 1 + PUSH : 1 + TOP, :], in_=Wa.rearrange("(j n) k -> n j k", n=P)
-        )
+        for j in (PUSH, POP, NOOP):
+            nc.sync.dma_start(out=operands[:, 1 + j, :], in_=Wa[j * P : (j + 1) * P, :])
         nc.sync.dma_start(out=operands[:, 1 + TOP, :], in_=Ws)
         nc.sync.dma_start(out=operands[:, 1 + OUT, :], in_=Wo)
         stack_sb = keep.tile([P, DEPTH, P], BF16)
         for bank in range(STACK_BANKS):
-            rows = slice(bank * SLICES_PER_BANK, (bank + 1) * SLICES_PER_BANK)
-            nc.sync.dma_start(out=stack_sb[:, rows, :], in_=stack[:, rows, :])
+            d_range = slice(bank * SLICES_PER_BANK, (bank + 1) * SLICES_PER_BANK)
+            nc.sync.dma_start(out=stack_sb[:, d_range, :], in_=stack[:, d_range, :])
 
         bias_rows = keep.tile([P, P], BF16)
         nc.vector.memset(bias_rows[:], 0.0)
@@ -67,12 +67,17 @@ def tile_stackrnn_pb_s_kernel(tc, h, stack, Wa, ba, Ws, bs, Wo, bo, out_0, out_1
         ident_bf16 = keep.tile([P, P], BF16)
         masks.make_identity(nc, ident_bf16[:])
 
+        rows = keep.tile([P, DEPTH + 2, P], F32)
+        nc.gpsimd.memset(rows[:, DEPTH + 1, :], -1.0)
+        step = keep.tile([P, STEPS, P], F32)
+
         grouped = keep.tile([P, OPERANDS, P, PACK], BF16, align_bytes=64)
         grouped_words = grouped[:].bitcast(F32)
         codes = keep.tile([P, OPERANDS * P], U32, align_bytes=64)
         scales = keep.tile([P, OPERANDS * P], U8, align_bytes=64)
-        for pair in range(PAIRS):
-            turned = psum_work.tile([P, 2, HALVES, P], F32, tag="work")
+
+        def turn_pair(pair):
+            turned = psum.tile([P, 2, HALVES, P], F32, tag="bank")
             for i in range(2):
                 words = operands[:, 2 * pair + i, :].bitcast(F32)
                 for u in range(HALVES):
@@ -85,12 +90,7 @@ def tile_stackrnn_pb_s_kernel(tc, h, stack, Wa, ba, Ws, bs, Wo, bo, out_0, out_1
                 in_=turned[:].rearrange("p i u r -> p i r u"),
             )
 
-        bias_turned = psum_work.tile([P, P], BF16, tag="work")
-        nc.tensor.transpose(out=bias_turned[:], in_=bias_rows[:], identity=ident_bf16[:])
-        bias = keep.tile([P, OUT + 1], F32)
-        nc.vector.tensor_copy(out=bias[:], in_=bias_turned[:, 0 : OUT + 1])
-
-        for pair in range(PAIRS):
+        def quantise_pair(pair):
             cols = slice(2 * pair * P, (2 * pair + 2) * P)
             nc.vector.quantize_mx(
                 out=codes[:, cols].bitcast(FP8X4),
@@ -98,8 +98,21 @@ def tile_stackrnn_pb_s_kernel(tc, h, stack, Wa, ba, Ws, bs, Wo, bo, out_0, out_1
                 in_=grouped[:, 2 * pair : 2 * pair + 2, :, :].rearrange("p o r t -> p (o r t)"),
             )
 
-        gates = psum_work.tile([P, TOP + 1, P], F32, tag="work")
-        readout = psum_work.tile([P, P], F32, tag="work")
+        turn_pair(0)
+        turn_pair(1)
+        quantise_pair(0)
+        bias_turned = psum.tile([P, P], BF16, tag="bank")
+        nc.tensor.transpose(out=bias_turned[:], in_=bias_rows[:], identity=ident_bf16[:])
+        bias = keep.tile([P, OUT + 1], F32)
+        nc.vector.tensor_copy(out=bias[:], in_=bias_turned[:, 0 : OUT + 1])
+        half_bs = keep.tile([P, 1], F32)
+        nc.vector.tensor_scalar_mul(out=half_bs[:], in0=bias[:, TOP : TOP + 1], scalar1=0.5)
+        quantise_pair(1)
+        turn_pair(2)
+        quantise_pair(2)
+
+        gates = psum.tile([P, TOP + 1, P], F32, tag="bank")
+        readout = psum.tile([P, P], F32, tag="bank")
         h_cols = slice(H_BLOCK * P, (H_BLOCK + 1) * P)
         for j in range(OUT + 1):
             w_cols = slice((1 + j) * P, (2 + j) * P)
@@ -113,10 +126,19 @@ def tile_stackrnn_pb_s_kernel(tc, h, stack, Wa, ba, Ws, bs, Wo, bo, out_0, out_1
                 stop=True,
             )
 
-        stack_turned_sb = keep.tile([P, DEPTH, P], BF16)
+        half_tanh = keep.tile([P, P], F32)
+        nc.scalar.activation(
+            out=half_tanh[:], in_=gates[:, TOP, :], func=ACT.Tanh, bias=half_bs[:], scale=0.5
+        )
+        nc.scalar.activation(out=rows[:, 0, :], in_=half_tanh[:], func=ACT.Copy, bias=0.5, scale=0.5)
+        out_turned = keep.tile([P, P], F32)
+        nc.scalar.activation(
+            out=out_turned[:], in_=readout[:], func=ACT.Identity, bias=bias[:, OUT : OUT + 1]
+        )
+
         stack_turned = []
         for bank in range(STACK_BANKS):
-            turned_bank = psum_stack.tile([P, SLICES_PER_BANK, P], BF16, name="stack_turned%d" % bank)
+            turned_bank = psum.tile([P, SLICES_PER_BANK, P], BF16, tag="bank", name="stack_turned%d" % bank)
             for i in range(SLICES_PER_BANK):
                 nc.tensor.transpose(
                     out=turned_bank[:, i, :],
@@ -125,15 +147,35 @@ def tile_stackrnn_pb_s_kernel(tc, h, stack, Wa, ba, Ws, bs, Wo, bo, out_0, out_1
                 )
             stack_turned.append(turned_bank)
 
-        def copy_turned_bank(bank):
-            rows = slice(bank * SLICES_PER_BANK, (bank + 1) * SLICES_PER_BANK)
-            nc.scalar.copy(out=stack_turned_sb[:, rows, :], in_=stack_turned[bank][:])
+        def widen_bank(bank):
+            first = 1 + bank * SLICES_PER_BANK
+            nc.scalar.copy(out=rows[:, first : first + SLICES_PER_BANK, :], in_=stack_turned[bank][:])
 
-        out_turned = keep.tile([P, P], F32)
-        nc.scalar.activation(
-            out=out_turned[:], in_=readout[:], func=ACT.Identity, bias=bias[:, OUT : OUT + 1]
-        )
-        copy_turned_bank(0)
+        def make_steps(piece):
+            lo = piece * CHUNK
+            hi = min(lo + CHUNK, STEPS)
+            nc.vector.tensor_sub(out=step[:, lo:hi, :], in0=rows[:, lo + 1 : hi + 1, :], in1=rows[:, lo:hi, :])
+
+        out_bank = psum.tile([P, P], F32, tag="bank")
+        nc.tensor.transpose(out=out_bank[:], in_=out_turned[:], identity=ident_f32[:])
+
+        blended = []
+
+        def turn_back(chunk, term, first_of_group, last_of_group):
+            for i in range(CHUNK):
+                nc.tensor.matmul(
+                    out=blended[chunk][:, i, :],
+                    lhsT=term[:, i, :],
+                    rhs=ident_f32[:],
+                    is_transpose=True,
+                    start=(first_of_group and i == 0),
+                    stop=(last_of_group and i == CHUNK - 1),
+                )
+
+        def open_chunk(chunk):
+            blended.append(psum.tile([P, CHUNK, P], F32, tag="bank", name="blended%d" % chunk))
+            first = chunk * CHUNK
+            turn_back(chunk, rows[:, first + 1 : first + 1 + CHUNK, :], True, False)
 
         logits = keep.tile([P, 3, P], F32)
         nc.vector.tensor_tensor(
@@ -143,82 +185,64 @@ def tile_stackrnn_pb_s_kernel(tc, h, stack, Wa, ba, Ws, bs, Wo, bo, out_0, out_1
             op=ALU.add,
         )
         peak = keep.tile([P, P], F32)
-        nc.vector.tensor_max(out=peak[:], in0=logits[:, PUSH, :], in1=logits[:, POP, :])
-        nc.vector.tensor_max(out=peak[:], in0=peak[:], in1=logits[:, NOOP, :])
+        nc.vector.tensor_reduce(
+            out=peak[:], in_=logits[:].rearrange("p j b -> p b j"), axis=AXIS.X, op=ALU.max
+        )
         nc.vector.tensor_tensor(
             out=logits[:],
             in0=logits[:],
             in1=peak[:].unsqueeze(1).to_broadcast([P, 3, P]),
             op=ALU.subtract,
         )
-        weight = keep.tile([P, 3, P], F32)
-        nc.scalar.activation(out=weight[:], in_=logits[:], func=ACT.Exp)
-        total = keep.tile([P, P], F32)
-        nc.vector.tensor_add(out=total[:], in0=weight[:, PUSH, :], in1=weight[:, POP, :])
-        nc.vector.tensor_add(out=total[:], in0=total[:], in1=weight[:, NOOP, :])
-        nc.vector.reciprocal(out=total[:], in_=total[:])
-        nc.vector.tensor_tensor(
-            out=weight[:],
-            in0=weight[:],
-            in1=total[:].unsqueeze(1).to_broadcast([P, 3, P]),
-            op=ALU.mult,
-        )
-
-        top = keep.tile([P, P], F32)
-        nc.scalar.activation(
-            out=top[:], in_=gates[:, TOP, :], func=ACT.Sigmoid, bias=bias[:, TOP : TOP + 1]
-        )
-        for bank in range(1, STACK_BANKS):
-            copy_turned_bank(bank)
-
-        out_bank = psum_work.tile([P, P], F32, tag="work")
-        nc.tensor.transpose(out=out_bank[:], in_=out_turned[:], identity=ident_f32[:])
+        widen_bank(0)
+        raised = keep.tile([P, 3, P], F32)
+        nc.scalar.activation(out=raised[:], in_=logits[:], func=ACT.Exp)
+        widen_bank(1)
         out_sb = keep.tile([P, P], F32)
         nc.scalar.copy(out=out_sb[:], in_=out_bank[:])
         nc.sync.dma_start(out=out_0, in_=out_sb[:])
+        widen_bank(2)
+        widen_bank(3)
+        for chunk in range(AHEAD):
+            open_chunk(chunk)
 
-        pushed = keep.tile([P, DEPTH + 1, P], F32)
-        popped = keep.tile([P, DEPTH + 1, P], F32)
-        stayed = keep.tile([P, DEPTH, P], F32)
-        nc.vector.tensor_mul(out=pushed[:, 0, :], in0=weight[:, PUSH, :], in1=top[:])
-        nc.vector.tensor_scalar_mul(out=popped[:, DEPTH, :], in0=weight[:, POP, :], scalar1=-1.0)
+        make_steps(0)
+        make_steps(1)
+        total = keep.tile([P, P], F32)
+        nc.vector.tensor_reduce(
+            out=total[:], in_=raised[:].rearrange("p j b -> p b j"), axis=AXIS.X, op=ALU.add
+        )
+        nc.vector.reciprocal(out=total[:], in_=total[:])
+        minus_push = keep.tile([P, P], F32)
+        nc.vector.scalar_tensor_tensor(
+            out=minus_push[:], in0=raised[:, PUSH, :], scalar=-1.0, in1=total[:], op0=ALU.mult, op1=ALU.mult
+        )
+        pop = keep.tile([P, P], F32)
+        nc.vector.tensor_mul(out=pop[:], in0=raised[:, POP, :], in1=total[:])
 
-        def multiply(product, first_slot, action, chunk):
-            if action == NOOP:
-                engine = nc.gpsimd
-                rows = stack_turned_sb[:, chunk * CHUNK : (chunk + 1) * CHUNK, :]
-            else:
-                engine = nc.vector
-                bank, half = divmod(chunk, SLICES_PER_BANK // CHUNK)
-                rows = stack_turned[bank][:, half * CHUNK : (half + 1) * CHUNK, :]
-            engine.tensor_tensor(
-                out=product[:, first_slot : first_slot + CHUNK, :],
-                in0=rows,
-                in1=weight[:, action, :].unsqueeze(1).to_broadcast([P, CHUNK, P]),
-                op=ALU.mult,
-            )
-
-        multiply(popped, 0, POP, 0)
+        pushed = keep.tile([P, DEPTH, P], F32)
+        popped = keep.tile([P, DEPTH, P], F32)
         for chunk in range(CHUNKS):
             first = chunk * CHUNK
-            multiply(stayed, first, NOOP, chunk)
-            multiply(pushed, first + 1, PUSH, chunk)
-            if chunk + 1 < CHUNKS:
-                multiply(popped, first + CHUNK, POP, chunk + 1)
-
-            blended = psum_work.tile([P, CHUNK, P], F32, tag="work")
-            for i in range(CHUNK):
-                d = first + i
-                terms = [popped[:, d + 1, :], stayed[:, d, :], pushed[:, d, :]]
-                for n, term in enumerate(terms):
-                    nc.tensor.matmul(
-                        out=blended[:, i, :],
-                        lhsT=term,
-                        rhs=ident_f32[:],
-                        is_transpose=True,
-                        start=(n == 0),
-                        stop=(n == len(terms) - 1),
-                    )
+            d_range = slice(first, first + CHUNK)
+            if (chunk + 2) * CHUNK < STEPS:
+                make_steps(chunk + 2)
+            nc.vector.tensor_tensor(
+                out=pushed[:, d_range, :],
+                in0=step[:, d_range, :],
+                in1=minus_push[:].unsqueeze(1).to_broadcast([P, CHUNK, P]),
+                op=ALU.mult,
+            )
+            nc.vector.tensor_tensor(
+                out=popped[:, d_range, :],
+                in0=step[:, first + 1 : first + 1 + CHUNK, :],
+                in1=pop[:].unsqueeze(1).to_broadcast([P, CHUNK, P]),
+                op=ALU.mult,
+            )
+            turn_back(chunk, pushed[:, d_range, :], False, False)
+            turn_back(chunk, popped[:, d_range, :], False, True)
+            if chunk + AHEAD < CHUNKS:
+                open_chunk(chunk + AHEAD)
             new_rows = staging.tile([P, CHUNK, P], F32)
-            nc.scalar.copy(out=new_rows[:], in_=blended[:])
-            nc.sync.dma_start(out=out_1[:, first : first + CHUNK, :], in_=new_rows[:])
+            nc.scalar.copy(out=new_rows[:], in_=blended[chunk][:])
+            nc.sync.dma_start(out=out_1[:, d_range, :], in_=new_rows[:])

@@ -26,9 +26,9 @@ PSUM_BANKS = 8
 SLICES_PER_BANK = 8
 STACK_BANKS = DEPTH // SLICES_PER_BANK
 CHUNK = 4
-CHUNKS = DEPTH // CHUNK
+TAIL = 2
 STEPS = DEPTH + 1
-AHEAD = 4
+AHEAD = 6
 
 FLOPS = 2 * P * HDIM * (3 * P + P + P)
 
@@ -36,7 +36,6 @@ FLOPS = 2 * P * HDIM * (3 * P + P + P)
 def tile_stackrnn_pb_s_kernel(tc, h, stack, Wa, ba, Ws, bs, Wo, bo, out_0, out_1):
     nc = tc.nc
     with ExitStack() as ctx:
-        ctx.enter_context(tc.manual_schedule())
         keep = ctx.enter_context(tc.tile_pool(name="keep", bufs=1))
         staging = ctx.enter_context(tc.tile_pool(name="staging", bufs=4))
         psum = ctx.enter_context(tc.psum_pool(name="psum", bufs=PSUM_BANKS))
@@ -159,90 +158,106 @@ def tile_stackrnn_pb_s_kernel(tc, h, stack, Wa, ba, Ws, bs, Wo, bo, out_0, out_1
         out_bank = psum.tile([P, P], F32, tag="bank")
         nc.tensor.transpose(out=out_bank[:], in_=out_turned[:], identity=ident_f32[:])
 
+        chunks = [(first, CHUNK) for first in range(0, DEPTH - CHUNK, CHUNK)]
+        chunks += [(DEPTH - CHUNK, TAIL), (DEPTH - TAIL, TAIL)]
         blended = []
 
-        def turn_back(chunk, term, first_of_group, last_of_group):
-            for i in range(CHUNK):
+        def turn_back(bank, term, first_of_group, last_of_group):
+            count = term.shape[1]
+            for i in range(count):
                 nc.tensor.matmul(
-                    out=blended[chunk][:, i, :],
+                    out=bank[:, i, :],
                     lhsT=term[:, i, :],
                     rhs=ident_f32[:],
                     is_transpose=True,
                     start=(first_of_group and i == 0),
-                    stop=(last_of_group and i == CHUNK - 1),
+                    stop=(last_of_group and i == count - 1),
                 )
 
-        def open_chunk(chunk):
-            blended.append(psum.tile([P, CHUNK, P], F32, tag="bank", name="blended%d" % chunk))
-            first = chunk * CHUNK
-            turn_back(chunk, rows[:, first + 1 : first + 1 + CHUNK, :], True, False)
+        def open_chunk(n):
+            first, count = chunks[n]
+            blended.append(psum.tile([P, count, P], F32, tag="bank", name="blended%d" % n))
+            turn_back(blended[n], rows[:, first + 1 : first + 1 + count, :], True, False)
 
+        halves = (slice(0, P // 2), slice(P // 2, P))
         logits = keep.tile([P, 3, P], F32)
-        nc.vector.tensor_tensor(
-            out=logits[:],
-            in0=gates[:, PUSH : NOOP + 1, :],
-            in1=bias[:, PUSH : NOOP + 1].unsqueeze(2).to_broadcast([P, 3, P]),
-            op=ALU.add,
-        )
+        for cols in halves:
+            nc.vector.tensor_tensor(
+                out=logits[:, :, cols],
+                in0=gates[:, PUSH : NOOP + 1, cols],
+                in1=bias[:, PUSH : NOOP + 1].unsqueeze(2).to_broadcast([P, 3, P // 2]),
+                op=ALU.add,
+            )
         peak = keep.tile([P, P], F32)
-        nc.vector.tensor_reduce(
-            out=peak[:], in_=logits[:].rearrange("p j b -> p b j"), axis=AXIS.X, op=ALU.max
-        )
-        nc.vector.tensor_tensor(
-            out=logits[:],
-            in0=logits[:],
-            in1=peak[:].unsqueeze(1).to_broadcast([P, 3, P]),
-            op=ALU.subtract,
-        )
+        for cols in halves:
+            nc.vector.tensor_reduce(
+                out=peak[:, cols], in_=logits[:, :, cols].rearrange("p j b -> p b j"), axis=AXIS.X, op=ALU.max
+            )
+        for cols in halves:
+            nc.vector.tensor_tensor(
+                out=logits[:, :, cols],
+                in0=logits[:, :, cols],
+                in1=peak[:, cols].unsqueeze(1).to_broadcast([P, 3, P // 2]),
+                op=ALU.subtract,
+            )
         widen_bank(0)
         raised = keep.tile([P, 3, P], F32)
-        nc.scalar.activation(out=raised[:], in_=logits[:], func=ACT.Exp)
+        for cols in halves:
+            nc.scalar.activation(out=raised[:, :, cols], in_=logits[:, :, cols], func=ACT.Exp)
         widen_bank(1)
         out_sb = keep.tile([P, P], F32)
         nc.scalar.copy(out=out_sb[:], in_=out_bank[:])
         nc.sync.dma_start(out=out_0, in_=out_sb[:])
         widen_bank(2)
         widen_bank(3)
-        for chunk in range(AHEAD):
-            open_chunk(chunk)
+        for n in range(AHEAD):
+            open_chunk(n)
 
         make_steps(0)
         make_steps(1)
         total = keep.tile([P, P], F32)
-        nc.vector.tensor_reduce(
-            out=total[:], in_=raised[:].rearrange("p j b -> p b j"), axis=AXIS.X, op=ALU.add
-        )
-        nc.vector.reciprocal(out=total[:], in_=total[:])
+        for cols in halves:
+            nc.vector.tensor_reduce(
+                out=total[:, cols], in_=raised[:, :, cols].rearrange("p j b -> p b j"), axis=AXIS.X, op=ALU.add
+            )
+        for cols in halves:
+            nc.vector.reciprocal(out=total[:, cols], in_=total[:, cols])
         minus_push = keep.tile([P, P], F32)
-        nc.vector.scalar_tensor_tensor(
-            out=minus_push[:], in0=raised[:, PUSH, :], scalar=-1.0, in1=total[:], op0=ALU.mult, op1=ALU.mult
-        )
+        for cols in halves:
+            nc.vector.scalar_tensor_tensor(
+                out=minus_push[:, cols],
+                in0=raised[:, PUSH, cols],
+                scalar=-1.0,
+                in1=total[:, cols],
+                op0=ALU.mult,
+                op1=ALU.mult,
+            )
         pop = keep.tile([P, P], F32)
-        nc.vector.tensor_mul(out=pop[:], in0=raised[:, POP, :], in1=total[:])
+        for cols in halves:
+            nc.vector.tensor_mul(out=pop[:, cols], in0=raised[:, POP, cols], in1=total[:, cols])
 
         pushed = keep.tile([P, DEPTH, P], F32)
         popped = keep.tile([P, DEPTH, P], F32)
-        for chunk in range(CHUNKS):
-            first = chunk * CHUNK
-            d_range = slice(first, first + CHUNK)
-            if (chunk + 2) * CHUNK < STEPS:
-                make_steps(chunk + 2)
+        for n, (first, count) in enumerate(chunks):
+            d_range = slice(first, first + count)
+            if (n + 2) * CHUNK < STEPS:
+                make_steps(n + 2)
             nc.vector.tensor_tensor(
                 out=pushed[:, d_range, :],
                 in0=step[:, d_range, :],
-                in1=minus_push[:].unsqueeze(1).to_broadcast([P, CHUNK, P]),
+                in1=minus_push[:].unsqueeze(1).to_broadcast([P, count, P]),
                 op=ALU.mult,
             )
             nc.vector.tensor_tensor(
                 out=popped[:, d_range, :],
-                in0=step[:, first + 1 : first + 1 + CHUNK, :],
-                in1=pop[:].unsqueeze(1).to_broadcast([P, CHUNK, P]),
+                in0=step[:, first + 1 : first + 1 + count, :],
+                in1=pop[:].unsqueeze(1).to_broadcast([P, count, P]),
                 op=ALU.mult,
             )
-            turn_back(chunk, pushed[:, d_range, :], False, False)
-            turn_back(chunk, popped[:, d_range, :], False, True)
-            if chunk + AHEAD < CHUNKS:
-                open_chunk(chunk + AHEAD)
-            new_rows = staging.tile([P, CHUNK, P], F32)
-            nc.scalar.copy(out=new_rows[:], in_=blended[chunk][:])
+            turn_back(blended[n], pushed[:, d_range, :], False, False)
+            turn_back(blended[n], popped[:, d_range, :], False, True)
+            if n + AHEAD < len(chunks):
+                open_chunk(n + AHEAD)
+            new_rows = staging.tile([P, count, P], F32, tag="new_rows")
+            nc.scalar.copy(out=new_rows[:], in_=blended[n][:])
             nc.sync.dma_start(out=out_1[:, d_range, :], in_=new_rows[:])

@@ -36,6 +36,7 @@ FLOPS = 2 * P * HDIM * (3 * P + P + P)
 def tile_stackrnn_pb_s_kernel(tc, h, stack, Wa, ba, Ws, bs, Wo, bo, out_0, out_1):
     nc = tc.nc
     with ExitStack() as ctx:
+        ctx.enter_context(tc.manual_schedule())
         keep = ctx.enter_context(tc.tile_pool(name="keep", bufs=1))
         staging = ctx.enter_context(tc.tile_pool(name="staging", bufs=4))
         psum = ctx.enter_context(tc.psum_pool(name="psum", bufs=PSUM_BANKS))

from contextlib import ExitStack

import concourse.masks as masks
import concourse.mybir as mybir

F32 = mybir.dt.float32
BF16 = mybir.dt.bfloat16
U32 = mybir.dt.uint32
U8 = mybir.dt.uint8
FP8X4 = mybir.dt.float8_e4m3fn_x4
ACT = mybir.ActivationFunctionType
ALU = mybir.AluOpType
AXIS = mybir.AxisListType

P = 128
HDIM = 512
DEPTH = 32
HALVES = 2
PACK = 4

H_BLOCK = 0
PUSH, POP, NOOP, TOP, OUT = 0, 1, 2, 3, 4
OPERANDS = 6

PSUM_BANKS = 8
SLICES_PER_BANK = 8
STACK_BANKS = DEPTH // SLICES_PER_BANK
CHUNK = 4
TAIL = 2
STEPS = DEPTH + 1
AHEAD = 6

FLOPS = 2 * P * HDIM * (3 * P + P + P)


def tile_stackrnn_pb_s_kernel(tc, h, stack, Wa, ba, Ws, bs, Wo, bo, out_0, out_1):
    nc = tc.nc
    with ExitStack() as ctx:
        ctx.enter_context(tc.manual_schedule())
        keep = ctx.enter_context(tc.tile_pool(name="keep", bufs=1))
        staging = ctx.enter_context(tc.tile_pool(name="staging", bufs=4))
        psum = ctx.enter_context(tc.psum_pool(name="psum", bufs=PSUM_BANKS))

        operands = keep.tile([P, OPERANDS, HDIM], BF16)
        nc.sync.dma_start(out=operands[:, H_BLOCK, :], in_=h)
        for j in (PUSH, POP, NOOP):
            nc.sync.dma_start(out=operands[:, 1 + j, :], in_=Wa[j * P : (j + 1) * P, :])
        nc.sync.dma_start(out=operands[:, 1 + TOP, :], in_=Ws)
        nc.sync.dma_start(out=operands[:, 1 + OUT, :], in_=Wo)
        stack_sb = keep.tile([P, DEPTH, P], BF16)
        for bank in range(STACK_BANKS):
            d_range = slice(bank * SLICES_PER_BANK, (bank + 1) * SLICES_PER_BANK)
            nc.sync.dma_start(out=stack_sb[:, d_range, :], in_=stack[:, d_range, :])

        bias_rows = keep.tile([P, P], BF16)
        nc.vector.memset(bias_rows[:], 0.0)
        nc.scalar.dma_start(out=bias_rows[PUSH : NOOP + 1, :], in_=ba.rearrange("(j n) -> j n", n=P))
        nc.scalar.dma_start(out=bias_rows[TOP : TOP + 1, :], in_=bs.rearrange("(o n) -> o n", o=1))
        nc.scalar.dma_start(out=bias_rows[OUT : OUT + 1, :], in_=bo.rearrange("(o n) -> o n", o=1))

        warm = keep.tile([P, 1], F32)
        nc.vector.memset(warm[:], 0.0)
        nc.scalar.activation(out=warm[:], in_=warm[:], func=ACT.Exp)

        ident_f32 = keep.tile([P, P], F32)
        masks.make_identity(nc, ident_f32[:])
        ident_bf16 = keep.tile([P, P], BF16)
        masks.make_identity(nc, ident_bf16[:])

        rows = keep.tile([P, DEPTH + 2, P], F32)
        nc.gpsimd.memset(rows[:, DEPTH + 1, :], -1.0)
        step = keep.tile([P, STEPS, P], F32)

        grouped = keep.tile([P, OPERANDS, P, PACK], BF16, align_bytes=64)
        grouped_words = grouped[:].bitcast(F32)
        codes = keep.tile([P, OPERANDS * P], U32, align_bytes=64)
        scales = keep.tile([P, OPERANDS * P], U8, align_bytes=64)

        def turn_pair(pair):
            turned = psum.tile([P, 2, HALVES, P], F32, tag="bank")
            for i in range(2):
                words = operands[:, 2 * pair + i, :].bitcast(F32)
                for u in range(HALVES):
                    nc.tensor.transpose(
                        out=turned[:, i, u, :], in_=words[:, u * P : (u + 1) * P], identity=ident_f32[:]
                    )
            copy_out = nc.scalar.copy if pair % 2 == 0 else nc.vector.tensor_copy
            copy_out(
                out=grouped_words[:, 2 * pair : 2 * pair + 2, :, :],
                in_=turned[:].rearrange("p i u r -> p i r u"),
            )

        def quantise_pair(pair):
            cols = slice(2 * pair * P, (2 * pair + 2) * P)
            nc.vector.quantize_mx(
                out=codes[:, cols].bitcast(FP8X4),
                scales=scales[:, cols],
                in_=grouped[:, 2 * pair : 2 * pair + 2, :, :].rearrange("p o r t -> p (o r t)"),
            )

        turn_pair(0)
        turn_pair(1)
        quantise_pair(0)
        bias_turned = psum.tile([P, P], BF16, tag="bank")
        nc.tensor.transpose(out=bias_turned[:], in_=bias_rows[:], identity=ident_bf16[:])
        bias = keep.tile([P, OUT + 1], F32)
        nc.vector.tensor_copy(out=bias[:], in_=bias_turned[:, 0 : OUT + 1])
        half_bs = keep.tile([P, 1], F32)
        nc.vector.tensor_scalar_mul(out=half_bs[:], in0=bias[:, TOP : TOP + 1], scalar1=0.5)
        quantise_pair(1)
        turn_pair(2)
        quantise_pair(2)

        gates = psum.tile([P, TOP + 1, P], F32, tag="bank")
        readout = psum.tile([P, P], F32, tag="bank")
        h_cols = slice(H_BLOCK * P, (H_BLOCK + 1) * P)
        for j in range(OUT + 1):
            w_cols = slice((1 + j) * P, (2 + j) * P)
            nc.tensor.matmul_mx(
                out=readout[:] if j == OUT else gates[:, j, :],
                lhsT=codes[:, w_cols].bitcast(FP8X4),
                lhsT_scale=scales[:, w_cols],
                rhs=codes[:, h_cols].bitcast(FP8X4),
                rhs_scale=scales[:, h_cols],
                start=True,
                stop=True,
            )

        half_tanh = keep.tile([P, P], F32)
        nc.scalar.activation(
            out=half_tanh[:], in_=gates[:, TOP, :], func=ACT.Tanh, bias=half_bs[:], scale=0.5
        )
        nc.scalar.activation(out=rows[:, 0, :], in_=half_tanh[:], func=ACT.Copy, bias=0.5, scale=0.5)
        out_turned = keep.tile([P, P], F32)
        nc.scalar.activation(
            out=out_turned[:], in_=readout[:], func=ACT.Identity, bias=bias[:, OUT : OUT + 1]
        )

        stack_turned = []
        for bank in range(STACK_BANKS):
            turned_bank = psum.tile([P, SLICES_PER_BANK, P], BF16, tag="bank", name="stack_turned%d" % bank)
            for i in range(SLICES_PER_BANK):
                nc.tensor.transpose(
                    out=turned_bank[:, i, :],
                    in_=stack_sb[:, bank * SLICES_PER_BANK + i, :],
                    identity=ident_bf16[:],
                )
            stack_turned.append(turned_bank)

        def widen_bank(bank):
            first = 1 + bank * SLICES_PER_BANK
            nc.scalar.copy(out=rows[:, first : first + SLICES_PER_BANK, :], in_=stack_turned[bank][:])

        def make_steps(piece):
            lo = piece * CHUNK
            hi = min(lo + CHUNK, STEPS)
            nc.vector.tensor_sub(out=step[:, lo:hi, :], in0=rows[:, lo + 1 : hi + 1, :], in1=rows[:, lo:hi, :])

        out_bank = psum.tile([P, P], F32, tag="bank")
        nc.tensor.transpose(out=out_bank[:], in_=out_turned[:], identity=ident_f32[:])

        chunks = [(first, CHUNK) for first in range(0, DEPTH - CHUNK, CHUNK)]
        chunks += [(DEPTH - CHUNK, TAIL), (DEPTH - TAIL, TAIL)]
        blended = []

        def turn_back(bank, term, first_of_group, last_of_group):
            count = term.shape[1]
            for i in range(count):
                nc.tensor.matmul(
                    out=bank[:, i, :],
                    lhsT=term[:, i, :],
                    rhs=ident_f32[:],
                    is_transpose=True,
                    start=(first_of_group and i == 0),
                    stop=(last_of_group and i == count - 1),
                )

        def open_chunk(n):
            first, count = chunks[n]
            blended.append(psum.tile([P, count, P], F32, tag="bank", name="blended%d" % n))
            turn_back(blended[n], rows[:, first + 1 : first + 1 + count, :], True, False)

        halves = (slice(0, P // 2), slice(P // 2, P))
        logits = keep.tile([P, 3, P], F32)
        for cols in halves:
            nc.vector.tensor_tensor(
                out=logits[:, :, cols],
                in0=gates[:, PUSH : NOOP + 1, cols],
                in1=bias[:, PUSH : NOOP + 1].unsqueeze(2).to_broadcast([P, 3, P // 2]),
                op=ALU.add,
            )
        peak = keep.tile([P, P], F32)
        for cols in halves:
            nc.vector.tensor_reduce(
                out=peak[:, cols], in_=logits[:, :, cols].rearrange("p j b -> p b j"), axis=AXIS.X, op=ALU.max
            )
        for cols in halves:
            nc.vector.tensor_tensor(
                out=logits[:, :, cols],
                in0=logits[:, :, cols],
                in1=peak[:, cols].unsqueeze(1).to_broadcast([P, 3, P // 2]),
                op=ALU.subtract,
            )
        widen_bank(0)
        raised = keep.tile([P, 3, P], F32)
        for cols in halves:
            nc.scalar.activation(out=raised[:, :, cols], in_=logits[:, :, cols], func=ACT.Exp)
        widen_bank(1)
        out_sb = keep.tile([P, P], F32)
        nc.scalar.copy(out=out_sb[:], in_=out_bank[:])
        nc.sync.dma_start(out=out_0, in_=out_sb[:])
        widen_bank(2)
        widen_bank(3)
        for n in range(AHEAD):
            open_chunk(n)

        make_steps(0)
        make_steps(1)
        total = keep.tile([P, P], F32)
        for cols in halves:
            nc.vector.tensor_reduce(
                out=total[:, cols], in_=raised[:, :, cols].rearrange("p j b -> p b j"), axis=AXIS.X, op=ALU.add
            )
        for cols in halves:
            nc.vector.reciprocal(out=total[:, cols], in_=total[:, cols])
        minus_push = keep.tile([P, P], F32)
        for cols in halves:
            nc.vector.scalar_tensor_tensor(
                out=minus_push[:, cols],
                in0=raised[:, PUSH, cols],
                scalar=-1.0,
                in1=total[:, cols],
                op0=ALU.mult,
                op1=ALU.mult,
            )
        pop = keep.tile([P, P], F32)
        for cols in halves:
            nc.vector.tensor_mul(out=pop[:, cols], in0=raised[:, POP, cols], in1=total[:, cols])

        pushed = keep.tile([P, DEPTH, P], F32)
        popped = keep.tile([P, DEPTH, P], F32)
        for n, (first, count) in enumerate(chunks):
            d_range = slice(first, first + count)
            if (n + 2) * CHUNK < STEPS:
                make_steps(n + 2)
            nc.vector.tensor_tensor(
                out=pushed[:, d_range, :],
                in0=step[:, d_range, :],
                in1=minus_push[:].unsqueeze(1).to_broadcast([P, count, P]),
                op=ALU.mult,
            )
            nc.vector.tensor_tensor(
                out=popped[:, d_range, :],
                in0=step[:, first + 1 : first + 1 + count, :],
                in1=pop[:].unsqueeze(1).to_broadcast([P, count, P]),
                op=ALU.mult,
            )
            turn_back(blended[n], pushed[:, d_range, :], False, False)
            turn_back(blended[n], popped[:, d_range, :], False, True)
            if n + AHEAD < len(chunks):
                open_chunk(n + AHEAD)
            new_rows = staging.tile([P, count, P], F32, tag="new_rows")
            nc.scalar.copy(out=new_rows[:], in_=blended[n][:])
            nc.sync.dma_start(out=out_1[:, d_range, :], in_=new_rows[:])
